import numpy as np
import ml_dtypes


def mxq(x, axis, fmt="e4m3"):
    dtype, down = {"e4m3": (ml_dtypes.float8_e4m3fn, 7), "e5m2": (ml_dtypes.float8_e5m2, 14)}[fmt]
    v = np.moveaxis(np.asarray(x, np.float32).astype(ml_dtypes.bfloat16).astype(np.float64), axis, -1)
    blocks = v.reshape(v.shape[:-1] + (-1, 32))
    amax = np.abs(blocks).max(-1, keepdims=True)
    byte = np.maximum(np.where(amax > 0, np.frexp(amax)[1] - 1 + 127, 0) - down, 1)
    scale = np.exp2(byte - 127.0)
    codes = (blocks / scale).astype(np.float32).astype(dtype).astype(np.float64)
    return np.moveaxis((codes * scale).reshape(v.shape), -1, axis)


WIDE = False


def mx_kscale(k):
    if not WIDE:
        return np.ones(k)
    levels = np.array([10, -10, 5, -5, 0])
    a = np.random.permutation(np.resize(levels, k // 512 * 4)).reshape(k // 512, 4)
    idx = np.arange(k)
    return np.exp2(a[idx // 512, idx % 128 // 32])


BF16 = ml_dtypes.bfloat16


def bf(x):
    return np.asarray(x, np.float32).astype(BF16)


def f64(x):
    return np.asarray(x).astype(np.float64)


NB, C, O, CZ, DD, HH, WW, MG = 1, 1024, 128, 128, 8, 16, 16, 4
STRIDES = (2, 2, 2)


def setup_inputs():
    s = mx_kscale(C)
    sd, sh, sw = STRIDES
    return {"x": bf(np.random.standard_normal((NB, C, DD, HH, WW)) * s[None, :, None, None, None]),
            "z": bf(np.random.standard_normal((NB, CZ, sd * DD + MG, sh * HH + MG, sw * WW + MG))),
            "W": bf(np.random.standard_normal((O, C)) / np.sqrt(C) / s[None, :]),
            "b": bf(np.random.standard_normal(O) * 0.5)}


def reference(x, z, W, b):
    sd, sh, sw = STRIDES
    u = np.repeat(np.repeat(np.repeat(f64(x), sd, axis=2), sh, axis=3), sw, axis=4)
    n, c, d, h, w = u.shape
    y = mxq(f64(W), 1, "e4m3") @ mxq(u.reshape(n, c, d * h * w), 1, "e4m3")
    y = y.reshape(n, -1, d, h, w) + f64(b)[None, :, None, None, None]
    zf = f64(z)
    off = [(zf.shape[i] - y.shape[i]) // 2 for i in range(2, 5)]
    zc = zf[:, :,
            off[0]:off[0] + y.shape[2],
            off[1]:off[1] + y.shape[3],
            off[2]:off[2] + y.shape[4]]
    return np.concatenate([y, zc], axis=1)

@@ -1,0 +1,159 @@
+import concourse.mybir as mybir
+from concourse.masks import make_identity
+
+F32 = mybir.dt.float32
+BF16 = mybir.dt.bfloat16
+U32 = mybir.dt.uint32
+U8 = mybir.dt.uint8
+FP8X4 = mybir.dt.float8_e4m3fn_x4
+IDENTITY = mybir.ActivationFunctionType.Identity
+
+P = 128
+PACK = 4
+K_PASS = P * PACK
+C_IN = 1024
+PASSES = C_IN // K_PASS
+C_OUT = 128
+D_IN, H_IN, W_IN = 8, 16, 16
+POS = D_IN * H_IN * W_IN
+SLICE = H_IN * W_IN
+CHUNK = 2 * SLICE
+N_CHUNKS = POS // CHUNK
+Z_SIDE = 36
+MARGIN = 2
+OUT_D, OUT_H, OUT_W = 16, 32, 32
+D_TILE = 4
+
+FLOPS = 2 * C_OUT * C_IN * OUT_D * OUT_H * OUT_W
+BYTES = (C_IN * POS * 2 + C_OUT * OUT_D * OUT_H * OUT_W * 2 + C_OUT * C_IN * 2 + C_OUT * 2
+         + 2 * C_OUT * OUT_D * OUT_H * OUT_W * 4)
+
+
+def tile_upconvcropcat_t_kernel(tc, x, z, W, b, out):
+    nc = tc.nc
+    x_rows = x[0].rearrange("c d h w -> c (d h w)")
+
+    with tc.tile_pool(name="consts", bufs=1) as consts, \
+            tc.tile_pool(name="xin", bufs=1) as xin, \
+            tc.tile_pool(name="zin", bufs=1) as zin, \
+            tc.tile_pool(name="grp", bufs=4) as grp, \
+            tc.tile_pool(name="mx", bufs=1) as mx, \
+            tc.tile_pool(name="ostage", bufs=6) as ostage, \
+            tc.psum_pool(name="psum", bufs=8) as psum:
+
+        w_sb = consts.tile([P, C_IN], BF16, name="w_sb")
+        nc.scalar.dma_start(out=w_sb[:], in_=W)
+        b_row = consts.tile([1, C_OUT], BF16, name="b_row")
+        nc.scalar.dma_start(out=b_row[:], in_=b.unsqueeze(0))
+
+        z_raw = [zin.tile([P, D_TILE, Z_SIDE, Z_SIDE], BF16, name="z_raw%d" % i) for i in range(4)]
+        x_raw = [xin.tile([P, PACK, POS], BF16, name="x_raw%d" % g) for g in range(PASSES)]
+
+        def load_z(i):
+            d0 = MARGIN + D_TILE * i
+            nc.sync.dma_start(out=z_raw[i][:], in_=z[0, :, d0:d0 + D_TILE, :, :])
+
+        def load_x(g):
+            nc.sync.dma_start(
+                out=x_raw[g][:],
+                in_=x_rows[K_PASS * g:K_PASS * (g + 1), :].rearrange("(p j) n -> p j n", j=PACK))
+
+        load_z(0)
+        load_z(1)
+        load_x(0)
+        load_x(1)
+        load_z(2)
+        load_z(3)
+
+        ident = consts.tile([P, P], F32, name="ident")
+        make_identity(nc, ident[:])
+        w_words = w_sb[:].bitcast(F32).rearrange("o (g p u) -> o g u p", g=PASSES, u=2)
+        w_ps = psum.tile([P, PASSES, 2, C_OUT], F32, name="w_ps", tag="bank")
+        for g in range(PASSES):
+            for u in range(2):
+                nc.tensor.transpose(w_ps[:, g, u, :], w_words[:, g, u, :], ident[:])
+        w_grouped = consts.tile([P, PASSES * C_OUT * PACK], BF16, name="w_grouped", align_bytes=64)
+        nc.vector.tensor_copy(
+            out=w_grouped[:].bitcast(F32).rearrange("p (g o u) -> p g o u", g=PASSES, u=2),
+            in_=w_ps[:].rearrange("p g u o -> p g o u"))
+        w_codes = consts.tile([P, PASSES * C_OUT], U32, name="w_codes", align_bytes=64)
+        w_scales = consts.tile([P, PASSES * C_OUT], U8, name="w_scales", align_bytes=64)
+
+        b_sq = consts.tile([P, P], F32, name="b_sq")
+        nc.vector.memset(b_sq[:], 0.0)
+        nc.vector.tensor_copy(out=b_sq[0:1, :], in_=b_row[:])
+        b_ps = psum.tile([P, 4 * P], F32, name="b_ps", tag="bank")
+        nc.tensor.transpose(b_ps[:, 0:P], b_sq[:], ident[:])
+        bias = consts.tile([P, 1], F32, name="bias")
+        nc.vector.tensor_copy(out=bias[:], in_=b_ps[:, 0:1])
+
+        nc.vector.quantize_mx(out=w_codes[:].bitcast(FP8X4), scales=w_scales[:], in_=w_grouped[:])
+
+        def crop_z(i):
+            zt = ostage.tile([P, D_TILE, OUT_H, OUT_W], F32, name="zt", tag="ostage")
+            nc.vector.tensor_copy(
+                out=zt[:],
+                in_=z_raw[i][:, :, MARGIN:MARGIN + OUT_H, MARGIN:MARGIN + OUT_W])
+            nc.sync.dma_start(out=out[0, C_OUT:2 * C_OUT, D_TILE * i:D_TILE * (i + 1), :, :], in_=zt[:])
+
+        crop_z(0)
+        crop_z(1)
+
+        codes = [[mx.tile([P, CHUNK], U32, name="codes%d_%d" % (g, q), align_bytes=64)
+                  for q in range(N_CHUNKS)] for g in range(PASSES)]
+        scales = [[mx.tile([P, CHUNK], U8, name="scales%d_%d" % (g, q), align_bytes=64)
+                   for q in range(N_CHUNKS)] for g in range(PASSES)]
+
+        def regroup(g, q):
+            grouped = grp.tile([P, CHUNK, PACK], BF16, name="grouped", tag="grouped", align_bytes=64)
+            nc.vector.tensor_copy(
+                out=grouped[:].rearrange("p (c i) t -> p c t i", i=4),
+                in_=x_raw[g][:, :, CHUNK * q:CHUNK * (q + 1)].rearrange("p t (c i) -> p c t i", i=4))
+            return grouped
+
+        def quantise(g, q, grouped):
+            nc.vector.quantize_mx(
+                out=codes[g][q][:].bitcast(FP8X4),
+                scales=scales[g][q][:],
+                in_=grouped[:].rearrange("p n t -> p (n t)"))
+
+        waiting = None
+        for g in range(PASSES):
+            for q in range(N_CHUNKS):
+                grouped = regroup(g, q)
+                if waiting is not None:
+                    quantise(*waiting)
+                waiting = (g, q, grouped)
+        quantise(*waiting)
+
+        def conv(m):
+            yt = ostage.tile([P, D_TILE, OUT_H, OUT_W], F32, name="yt", tag="ostage")
+            for dl in range(2):
+                cols = slice(SLICE * dl, SLICE * (dl + 1))
+                for a in range(2):
+                    rows = yt[:, 2 * dl + a, :, :].rearrange("p (hh r) (ww c) -> p r hh ww c", r=2, c=2)
+                    for r in range(2):
+                        acc = psum.tile([P, 2, SLICE], F32, name="acc", tag="bank")
+                        for c in range(2):
+                            for g in range(PASSES):
+                                o_cols = slice(C_OUT * g, C_OUT * (g + 1))
+                                nc.tensor.matmul_mx(
+                                    out=acc[:, c, :],
+                                    lhsT=w_codes[:, o_cols].bitcast(FP8X4),
+                                    lhsT_scale=w_scales[:, o_cols],
+                                    rhs=codes[g][m][:, cols].bitcast(FP8X4),
+                                    rhs_scale=scales[g][m][:, cols],
+                                    start=(g == 0),
+                                    stop=(g == PASSES - 1))
+                        nc.scalar.activation(
+                            out=rows[:, r],
+                            in_=acc[:].rearrange("p c (hh ww) -> p hh ww c", ww=W_IN),
+                            func=IDENTITY, bias=bias[:, 0:1], scale=1.0)
+            nc.sync.dma_start(out=out[0, 0:C_OUT, D_TILE * m:D_TILE * (m + 1), :, :], in_=yt[:])
+
+        conv(0)
+        conv(1)
+        crop_z(2)
+        crop_z(3)
+        conv(2)
+        conv(3)

@@ -46,12 +46,12 @@ def tile_upconvcropcat_t_kernel(tc, x, z, W, b, out):
         b_row = consts.tile([1, C_OUT], BF16, name="b_row")
         nc.scalar.dma_start(out=b_row[:], in_=b.unsqueeze(0))
 
-        z_raw = [zin.tile([P, D_TILE, Z_SIDE, Z_SIDE], BF16, name="z_raw%d" % i) for i in range(4)]
+        z_raw = [zin.tile([P, D_TILE, OUT_H, Z_SIDE], BF16, name="z_raw%d" % i) for i in range(4)]
         x_raw = [xin.tile([P, PACK, POS], BF16, name="x_raw%d" % g) for g in range(PASSES)]
 
         def load_z(i):
             d0 = MARGIN + D_TILE * i
-            nc.sync.dma_start(out=z_raw[i][:], in_=z[0, :, d0:d0 + D_TILE, :, :])
+            nc.sync.dma_start(out=z_raw[i][:], in_=z[0, :, d0:d0 + D_TILE, MARGIN:MARGIN + OUT_H, :])
 
         def load_x(g):
             nc.sync.dma_start(
@@ -93,7 +93,7 @@ def tile_upconvcropcat_t_kernel(tc, x, z, W, b, out):
             zt = ostage.tile([P, D_TILE, OUT_H, OUT_W], F32, name="zt", tag="ostage")
             nc.vector.tensor_copy(
                 out=zt[:],
-                in_=z_raw[i][:, :, MARGIN:MARGIN + OUT_H, MARGIN:MARGIN + OUT_W])
+                in_=z_raw[i][:, :, :, MARGIN:MARGIN + OUT_W])
             nc.sync.dma_start(out=out[0, C_OUT:2 * C_OUT, D_TILE * i:D_TILE * (i + 1), :, :], in_=zt[:])
 
         crop_z(0)

@@ -36,34 +36,57 @@ def tile_upconvcropcat_t_kernel(tc, x, z, W, b, out):
     with tc.tile_pool(name="consts", bufs=1) as consts, \
             tc.tile_pool(name="xin", bufs=1) as xin, \
             tc.tile_pool(name="zin", bufs=1) as zin, \
-            tc.tile_pool(name="grp", bufs=4) as grp, \
+            tc.tile_pool(name="grp", bufs=8) as grp, \
             tc.tile_pool(name="mx", bufs=1) as mx, \
             tc.tile_pool(name="ostage", bufs=6) as ostage, \
-            tc.psum_pool(name="psum", bufs=8) as psum:
+            tc.psum_pool(name="psum", bufs=8) as psum, \
+            tc.manual_schedule():
 
         w_sb = consts.tile([P, C_IN], BF16, name="w_sb")
         nc.scalar.dma_start(out=w_sb[:], in_=W)
         b_row = consts.tile([1, C_OUT], BF16, name="b_row")
         nc.scalar.dma_start(out=b_row[:], in_=b.unsqueeze(0))
 
-        z_raw = [zin.tile([P, D_TILE, OUT_H, Z_SIDE], BF16, name="z_raw%d" % i) for i in range(4)]
         x_raw = [xin.tile([P, PACK, POS], BF16, name="x_raw%d" % g) for g in range(PASSES)]
-
-        def load_z(i):
-            d0 = MARGIN + D_TILE * i
-            nc.sync.dma_start(out=z_raw[i][:], in_=z[0, :, d0:d0 + D_TILE, MARGIN:MARGIN + OUT_H, :])
-
-        def load_x(g):
+        z_raw = [zin.tile([P, D_TILE, OUT_H, Z_SIDE], BF16, name="z_raw%d" % i) for i in range(4)]
+        for g in range(PASSES):
             nc.sync.dma_start(
                 out=x_raw[g][:],
                 in_=x_rows[K_PASS * g:K_PASS * (g + 1), :].rearrange("(p j) n -> p j n", j=PACK))
+        for i in range(4):
+            d0 = MARGIN + D_TILE * i
+            nc.sync.dma_start(out=z_raw[i][:], in_=z[0, :, d0:d0 + D_TILE, MARGIN:MARGIN + OUT_H, :])
 
-        load_z(0)
-        load_z(1)
-        load_x(0)
-        load_x(1)
-        load_z(2)
-        load_z(3)
+        codes = [[mx.tile([P, CHUNK], U32, name="codes%d_%d" % (g, q), align_bytes=64)
+                  for q in range(N_CHUNKS)] for g in range(PASSES)]
+        scales = [[mx.tile([P, CHUNK], U8, name="scales%d_%d" % (g, q), align_bytes=64)
+                   for q in range(N_CHUNKS)] for g in range(PASSES)]
+
+        def regroup(g, q, copy):
+            grouped = grp.tile([P, CHUNK, PACK], BF16, name="grouped", tag="grouped", align_bytes=64)
+            copy(
+                out=grouped[:].rearrange("p (c i) t -> p c t i", i=4),
+                in_=x_raw[g][:, :, CHUNK * q:CHUNK * (q + 1)].rearrange("p t (c i) -> p c t i", i=4))
+            return grouped
+
+        def quantise(g, q, grouped):
+            nc.vector.quantize_mx(
+                out=codes[g][q][:].bitcast(FP8X4),
+                scales=scales[g][q][:],
+                in_=grouped[:].rearrange("p n t -> p (n t)"))
+
+        def crop_z(i, copy):
+            zt = ostage.tile([P, D_TILE, OUT_H, OUT_W], F32, name="zt", tag="ostage")
+            copy(out=zt[:], in_=z_raw[i][:, :, :, MARGIN:MARGIN + OUT_W])
+            nc.sync.dma_start(out=out[0, C_OUT:2 * C_OUT, D_TILE * i:D_TILE * (i + 1), :, :], in_=zt[:])
+
+        on_vector = nc.vector.tensor_copy
+        on_scalar = nc.scalar.copy
+
+        g00 = regroup(0, 0, on_vector)
+        g01 = regroup(0, 1, on_vector)
+        g02 = regroup(0, 2, on_scalar)
+        g03 = regroup(0, 3, on_scalar)
 
         ident = consts.tile([P, P], F32, name="ident")
         make_identity(nc, ident[:])
@@ -89,42 +112,22 @@ def tile_upconvcropcat_t_kernel(tc, x, z, W, b, out):
 
         nc.vector.quantize_mx(out=w_codes[:].bitcast(FP8X4), scales=w_scales[:], in_=w_grouped[:])
 
-        def crop_z(i):
-            zt = ostage.tile([P, D_TILE, OUT_H, OUT_W], F32, name="zt", tag="ostage")
-            nc.vector.tensor_copy(
-                out=zt[:],
-                in_=z_raw[i][:, :, :, MARGIN:MARGIN + OUT_W])
-            nc.sync.dma_start(out=out[0, C_OUT:2 * C_OUT, D_TILE * i:D_TILE * (i + 1), :, :], in_=zt[:])
-
-        crop_z(0)
-        crop_z(1)
-
-        codes = [[mx.tile([P, CHUNK], U32, name="codes%d_%d" % (g, q), align_bytes=64)
-                  for q in range(N_CHUNKS)] for g in range(PASSES)]
-        scales = [[mx.tile([P, CHUNK], U8, name="scales%d_%d" % (g, q), align_bytes=64)
-                   for q in range(N_CHUNKS)] for g in range(PASSES)]
-
-        def regroup(g, q):
-            grouped = grp.tile([P, CHUNK, PACK], BF16, name="grouped", tag="grouped", align_bytes=64)
-            nc.vector.tensor_copy(
-                out=grouped[:].rearrange("p (c i) t -> p c t i", i=4),
-                in_=x_raw[g][:, :, CHUNK * q:CHUNK * (q + 1)].rearrange("p t (c i) -> p c t i", i=4))
-            return grouped
-
-        def quantise(g, q, grouped):
-            nc.vector.quantize_mx(
-                out=codes[g][q][:].bitcast(FP8X4),
-                scales=scales[g][q][:],
-                in_=grouped[:].rearrange("p n t -> p (n t)"))
-
-        waiting = None
-        for g in range(PASSES):
-            for q in range(N_CHUNKS):
-                grouped = regroup(g, q)
-                if waiting is not None:
-                    quantise(*waiting)
-                waiting = (g, q, grouped)
-        quantise(*waiting)
+        quantise(0, 0, g00)
+        quantise(0, 1, g01)
+        g10 = regroup(1, 0, on_vector)
+        g11 = regroup(1, 1, on_vector)
+        quantise(0, 2, g02)
+        quantise(0, 3, g03)
+        quantise(1, 0, g10)
+        quantise(1, 1, g11)
+        crop_z(0, on_scalar)
+        crop_z(1, on_scalar)
+        g12 = regroup(1, 2, on_vector)
+        g13 = regroup(1, 3, on_vector)
+        quantise(1, 2, g12)
+        quantise(1, 3, g13)
+        crop_z(2, on_vector)
+        crop_z(3, on_vector)
 
         def conv(m):
             yt = ostage.tile([P, D_TILE, OUT_H, OUT_W], F32, name="yt", tag="ostage")
@@ -151,9 +154,5 @@ def tile_upconvcropcat_t_kernel(tc, x, z, W, b, out):
                             func=IDENTITY, bias=bias[:, 0:1], scale=1.0)
             nc.sync.dma_start(out=out[0, 0:C_OUT, D_TILE * m:D_TILE * (m + 1), :, :], in_=yt[:])
 
-        conv(0)
-        conv(1)
-        crop_z(2)
-        crop_z(3)
-        conv(2)
-        conv(3)
+        for m in range(N_CHUNKS):
+            conv(m)

import concourse.mybir as mybir
from concourse.masks import make_identity

F32 = mybir.dt.float32
BF16 = mybir.dt.bfloat16
U32 = mybir.dt.uint32
U8 = mybir.dt.uint8
FP8X4 = mybir.dt.float8_e4m3fn_x4
IDENTITY = mybir.ActivationFunctionType.Identity

P = 128
PACK = 4
K_PASS = P * PACK
C_IN = 1024
PASSES = C_IN // K_PASS
C_OUT = 128
D_IN, H_IN, W_IN = 8, 16, 16
POS = D_IN * H_IN * W_IN
SLICE = H_IN * W_IN
CHUNK = 2 * SLICE
N_CHUNKS = POS // CHUNK
Z_SIDE = 36
MARGIN = 2
OUT_D, OUT_H, OUT_W = 16, 32, 32
D_TILE = 4

FLOPS = 2 * C_OUT * C_IN * OUT_D * OUT_H * OUT_W
BYTES = (C_IN * POS * 2 + C_OUT * OUT_D * OUT_H * OUT_W * 2 + C_OUT * C_IN * 2 + C_OUT * 2
         + 2 * C_OUT * OUT_D * OUT_H * OUT_W * 4)


def tile_upconvcropcat_t_kernel(tc, x, z, W, b, out):
    nc = tc.nc
    x_rows = x[0].rearrange("c d h w -> c (d h w)")

    with tc.tile_pool(name="consts", bufs=1) as consts, \
            tc.tile_pool(name="xin", bufs=1) as xin, \
            tc.tile_pool(name="zin", bufs=1) as zin, \
            tc.tile_pool(name="grp", bufs=8) as grp, \
            tc.tile_pool(name="mx", bufs=1) as mx, \
            tc.tile_pool(name="ostage", bufs=6) as ostage, \
            tc.psum_pool(name="psum", bufs=8) as psum, \
            tc.manual_schedule():

        w_sb = consts.tile([P, C_IN], BF16, name="w_sb")
        nc.scalar.dma_start(out=w_sb[:], in_=W)
        b_row = consts.tile([1, C_OUT], BF16, name="b_row")
        nc.scalar.dma_start(out=b_row[:], in_=b.unsqueeze(0))

        x_raw = [xin.tile([P, PACK, POS], BF16, name="x_raw%d" % g) for g in range(PASSES)]
        z_raw = [zin.tile([P, D_TILE, OUT_H, Z_SIDE], BF16, name="z_raw%d" % i) for i in range(4)]
        for g in range(PASSES):
            nc.sync.dma_start(
                out=x_raw[g][:],
                in_=x_rows[K_PASS * g:K_PASS * (g + 1), :].rearrange("(p j) n -> p j n", j=PACK))
        for i in range(4):
            d0 = MARGIN + D_TILE * i
            nc.sync.dma_start(out=z_raw[i][:], in_=z[0, :, d0:d0 + D_TILE, MARGIN:MARGIN + OUT_H, :])

        codes = [[mx.tile([P, CHUNK], U32, name="codes%d_%d" % (g, q), align_bytes=64)
                  for q in range(N_CHUNKS)] for g in range(PASSES)]
        scales = [[mx.tile([P, CHUNK], U8, name="scales%d_%d" % (g, q), align_bytes=64)
                   for q in range(N_CHUNKS)] for g in range(PASSES)]

        def regroup(g, q, copy):
            grouped = grp.tile([P, CHUNK, PACK], BF16, name="grouped", tag="grouped", align_bytes=64)
            copy(
                out=grouped[:].rearrange("p (c i) t -> p c t i", i=4),
                in_=x_raw[g][:, :, CHUNK * q:CHUNK * (q + 1)].rearrange("p t (c i) -> p c t i", i=4))
            return grouped

        def quantise(g, q, grouped):
            nc.vector.quantize_mx(
                out=codes[g][q][:].bitcast(FP8X4),
                scales=scales[g][q][:],
                in_=grouped[:].rearrange("p n t -> p (n t)"))

        def crop_z(i, copy):
            zt = ostage.tile([P, D_TILE, OUT_H, OUT_W], F32, name="zt", tag="ostage")
            copy(out=zt[:], in_=z_raw[i][:, :, :, MARGIN:MARGIN + OUT_W])
            nc.sync.dma_start(out=out[0, C_OUT:2 * C_OUT, D_TILE * i:D_TILE * (i + 1), :, :], in_=zt[:])

        on_vector = nc.vector.tensor_copy
        on_scalar = nc.scalar.copy

        g00 = regroup(0, 0, on_vector)
        g01 = regroup(0, 1, on_vector)
        g02 = regroup(0, 2, on_scalar)
        g03 = regroup(0, 3, on_scalar)

        ident = consts.tile([P, P], F32, name="ident")
        make_identity(nc, ident[:])
        w_words = w_sb[:].bitcast(F32).rearrange("o (g p u) -> o g u p", g=PASSES, u=2)
        w_ps = psum.tile([P, PASSES, 2, C_OUT], F32, name="w_ps", tag="bank")
        for g in range(PASSES):
            for u in range(2):
                nc.tensor.transpose(w_ps[:, g, u, :], w_words[:, g, u, :], ident[:])
        w_grouped = consts.tile([P, PASSES * C_OUT * PACK], BF16, name="w_grouped", align_bytes=64)
        nc.vector.tensor_copy(
            out=w_grouped[:].bitcast(F32).rearrange("p (g o u) -> p g o u", g=PASSES, u=2),
            in_=w_ps[:].rearrange("p g u o -> p g o u"))
        w_codes = consts.tile([P, PASSES * C_OUT], U32, name="w_codes", align_bytes=64)
        w_scales = consts.tile([P, PASSES * C_OUT], U8, name="w_scales", align_bytes=64)

        b_sq = consts.tile([P, P], F32, name="b_sq")
        nc.vector.memset(b_sq[:], 0.0)
        nc.vector.tensor_copy(out=b_sq[0:1, :], in_=b_row[:])
        b_ps = psum.tile([P, 4 * P], F32, name="b_ps", tag="bank")
        nc.tensor.transpose(b_ps[:, 0:P], b_sq[:], ident[:])
        bias = consts.tile([P, 1], F32, name="bias")
        nc.vector.tensor_copy(out=bias[:], in_=b_ps[:, 0:1])

        nc.vector.quantize_mx(out=w_codes[:].bitcast(FP8X4), scales=w_scales[:], in_=w_grouped[:])

        quantise(0, 0, g00)
        quantise(0, 1, g01)
        g10 = regroup(1, 0, on_vector)
        g11 = regroup(1, 1, on_vector)
        quantise(0, 2, g02)
        quantise(0, 3, g03)
        quantise(1, 0, g10)
        quantise(1, 1, g11)
        crop_z(0, on_scalar)
        crop_z(1, on_scalar)
        g12 = regroup(1, 2, on_vector)
        g13 = regroup(1, 3, on_vector)
        quantise(1, 2, g12)
        quantise(1, 3, g13)
        crop_z(2, on_vector)
        crop_z(3, on_vector)

        def conv(m):
            yt = ostage.tile([P, D_TILE, OUT_H, OUT_W], F32, name="yt", tag="ostage")
            for dl in range(2):
                cols = slice(SLICE * dl, SLICE * (dl + 1))
                for a in range(2):
                    rows = yt[:, 2 * dl + a, :, :].rearrange("p (hh r) (ww c) -> p r hh ww c", r=2, c=2)
                    for r in range(2):
                        acc = psum.tile([P, 2, SLICE], F32, name="acc", tag="bank")
                        for c in range(2):
                            for g in range(PASSES):
                                o_cols = slice(C_OUT * g, C_OUT * (g + 1))
                                nc.tensor.matmul_mx(
                                    out=acc[:, c, :],
                                    lhsT=w_codes[:, o_cols].bitcast(FP8X4),
                                    lhsT_scale=w_scales[:, o_cols],
                                    rhs=codes[g][m][:, cols].bitcast(FP8X4),
                                    rhs_scale=scales[g][m][:, cols],
                                    start=(g == 0),
                                    stop=(g == PASSES - 1))
                        nc.scalar.activation(
                            out=rows[:, r],
                            in_=acc[:].rearrange("p c (hh ww) -> p hh ww c", ww=W_IN),
                            func=IDENTITY, bias=bias[:, 0:1], scale=1.0)
            nc.sync.dma_start(out=out[0, 0:C_OUT, D_TILE * m:D_TILE * (m + 1), :, :], in_=yt[:])

        for m in range(N_CHUNKS):
            conv(m)
